import numpy as np
import ml_dtypes


def mxq(x, axis, fmt="e4m3"):
    dtype, down = {"e4m3": (ml_dtypes.float8_e4m3fn, 7), "e5m2": (ml_dtypes.float8_e5m2, 14)}[fmt]
    v = np.moveaxis(np.asarray(x, np.float32).astype(ml_dtypes.bfloat16).astype(np.float64), axis, -1)
    blocks = v.reshape(v.shape[:-1] + (-1, 32))
    amax = np.abs(blocks).max(-1, keepdims=True)
    byte = np.maximum(np.where(amax > 0, np.frexp(amax)[1] - 1 + 127, 0) - down, 1)
    scale = np.exp2(byte - 127.0)
    codes = (blocks / scale).astype(np.float32).astype(dtype).astype(np.float64)
    return np.moveaxis((codes * scale).reshape(v.shape), -1, axis)


WIDE = False


def mx_kscale(k):
    if not WIDE:
        return np.ones(k)
    levels = np.array([10, -10, 5, -5, 0])
    a = np.random.permutation(np.resize(levels, k // 512 * 4)).reshape(k // 512, 4)
    idx = np.arange(k)
    return np.exp2(a[idx // 512, idx % 128 // 32])


BF16 = ml_dtypes.bfloat16


def bf(x):
    return np.asarray(x, np.float32).astype(BF16)


def f64(x):
    return np.asarray(x).astype(np.float64)


B, C, Q, O, H, W = 4, 1024, 1024, 512, 32, 32
N = H * W
SIG = 1.75


def setup_inputs():
    s = mx_kscale(N).reshape(H, W)
    return {"x": bf(np.random.standard_normal((B, C, H, W)) / s),
            "query": bf(np.random.standard_normal((B, Q, H, W)) * SIG / np.sqrt(N) * s)}


def reference(x, query):
    xf = f64(x).reshape(B, C, N)
    qf = f64(query).reshape(B, Q, N)
    energy = mxq(qf, 2, "e4m3") @ mxq(xf, 2, "e4m3").transpose(0, 2, 1)
    energy_new = energy.max(-1, keepdims=True) - energy
    e = np.exp(energy_new - energy_new.max(-1, keepdims=True))
    return e / e.sum(-1, keepdims=True)

@@ -1,0 +1,144 @@
+from contextlib import ExitStack
+
+import concourse.bass as bass
+import concourse.mybir as mybir
+import concourse.tile as tile
+from concourse.masks import make_identity
+
+F32 = mybir.dt.float32
+BF16 = mybir.dt.bfloat16
+U32 = mybir.dt.uint32
+U8 = mybir.dt.uint8
+FP8X4 = mybir.dt.float8_e4m3fn_x4
+ALU = mybir.AluOpType
+ACT = mybir.ActivationFunctionType
+
+B = 4
+P = 128
+CH = 1024
+K = 1024
+FLOPS = 2 * B * CH * CH * K
+
+UNITS = 4 * B
+ROUNDS = 4 * B
+
+
+def tile_guided_cam_module_pa_t_kernel(tc, x, query, out):
+    nc = tc.nc
+    with ExitStack() as ctx:
+        const = ctx.enter_context(tc.tile_pool(name="const", bufs=1))
+        inp = ctx.enter_context(tc.tile_pool(name="inp", bufs=8))
+        grp_pool = ctx.enter_context(tc.tile_pool(name="grp", bufs=3))
+        code_pool = ctx.enter_context(tc.tile_pool(name="code", bufs=8))
+        e_pool = ctx.enter_context(tc.tile_pool(name="e", bufs=4))
+        small = ctx.enter_context(tc.tile_pool(name="small", bufs=8))
+        tps = ctx.enter_context(tc.psum_pool(name="tps", bufs=4))
+        eps = ctx.enter_context(tc.psum_pool(name="eps", bufs=4))
+
+        ident = const.tile([P, P], F32)
+        make_identity(nc, ident[:])
+
+        raws = {}
+        codes = {}
+        scales = {}
+
+        def load(i):
+            b, u = divmod(i, 4)
+            a = u % 2
+            raw = inp.tile([P, 4096], BF16)
+            if u < 2:
+                view = x[b].rearrange("(a p t) h w -> a p (t h w)", a=2, t=4)
+            else:
+                view = query[b].rearrange("(p a t) h w -> a p (t h w)", a=2, t=4)
+            nc.sync.dma_start(out=raw[:], in_=view[a])
+            raws[i] = raw
+
+        def prep(i):
+            rawf = raws[i][:].bitcast(F32)
+            grp = grp_pool.tile([P, 4096], BF16, align_bytes=64)
+            grpf = grp[:].bitcast(F32).rearrange("p (g c u) -> p g c u", g=2, u=2)
+            for t in range(4):
+                tp = tps.tile([P, 4, P], F32)
+                for j in range(4):
+                    lo = t * 512 + j * P
+                    nc.tensor.transpose(tp[:, j, :], rawf[:, lo:lo + P], ident[:])
+                src = tp[:].rearrange("p (g u) c -> p g c u", u=2)
+                dst = grpf[:, :, t * P:(t + 1) * P, :]
+                on_vector = (t % 2 == 1) if i < 4 else (t == 3)
+                if on_vector:
+                    nc.vector.tensor_copy(out=dst, in_=src)
+                else:
+                    nc.scalar.copy(out=dst, in_=src)
+            cod = code_pool.tile([P, 1024], U32, align_bytes=64)
+            scl = code_pool.tile([P, 1024], U8, align_bytes=64)
+            nc.vector.quantize_mx(out=cod[:].bitcast(FP8X4), scales=scl[:], in_=grp[:])
+            codes[i] = cod
+            scales[i] = scl
+
+        def soft(j):
+            b, r = divmod(j, 4)
+            out_rows = out[b].rearrange("(p m) c -> p m c", m=8)
+            e_sb = e_pool.tile([P, 2, CH], F32)
+            for mi in range(2):
+                m = 2 * r + mi
+                qi = 4 * b + 2 + m // 4
+                t = m % 4
+                banks = []
+                for h in range(2):
+                    xi = 4 * b + h
+                    ep = eps.tile([P, 512], F32)
+                    for g in range(2):
+                        lo = g * 512 + t * P
+                        nc.tensor.matmul_mx(
+                            out=ep[:],
+                            lhsT=codes[qi][:, lo:lo + P].bitcast(FP8X4),
+                            lhsT_scale=scales[qi][:, lo:lo + P],
+                            rhs=codes[xi][:, g * 512:(g + 1) * 512].bitcast(FP8X4),
+                            rhs_scale=scales[xi][:, g * 512:(g + 1) * 512],
+                            start=(g == 0),
+                            stop=(g == 1),
+                        )
+                    banks.append(ep)
+                mn0 = small.tile([P, 1], F32)
+                mn = small.tile([P, 1], F32)
+                sm = small.tile([P, 1], F32)
+                rc = small.tile([P, 1], F32)
+                nc.vector.tensor_scalar(
+                    out=e_sb[:, mi, 0:512].rearrange("p (c t) -> p c t", t=4),
+                    in0=banks[0][:].rearrange("p (t c) -> p c t", t=4),
+                    scalar1=1.0, scalar2=None, op0=ALU.mult, op1=ALU.min,
+                    accum_out=mn0[:],
+                )
+                nc.vector.tensor_scalar(
+                    out=e_sb[:, mi, 512:1024].rearrange("p (c t) -> p c t", t=4),
+                    in0=banks[1][:].rearrange("p (t c) -> p c t", t=4),
+                    scalar1=1.0, scalar2=mn0[:], op0=ALU.mult, op1=ALU.min,
+                    accum_out=mn[:],
+                )
+                nc.scalar.activation(
+                    out=e_sb[:, mi, :], in_=e_sb[:, mi, :], func=ACT.Exp,
+                    bias=mn[:], scale=-1.0, accum_out=sm[:],
+                )
+                nc.vector.reciprocal(rc[:], sm[:])
+                nc.gpsimd.tensor_scalar(
+                    out=e_sb[:, mi, :], in0=e_sb[:, mi, :],
+                    scalar1=rc[:], scalar2=0.0, op0=ALU.mult, op1=ALU.add,
+                )
+            nc.sync.dma_start(out=out_rows[:, 2 * r:2 * r + 2, :], in_=e_sb[:])
+
+        for i in range(8):
+            load(i)
+
+        def prep_and_refill(i):
+            if i < UNITS:
+                prep(i)
+                if i + 8 < UNITS:
+                    load(i + 8)
+
+        for i in range(3):
+            prep_and_refill(i)
+        soft(0)
+        prep_and_refill(3)
+        for j in range(1, ROUNDS):
+            prep_and_refill(j + 3)
+            soft(j)

@@ -1,8 +1,6 @@
 from contextlib import ExitStack
 
-import concourse.bass as bass
 import concourse.mybir as mybir
-import concourse.tile as tile
 from concourse.masks import make_identity
 
 F32 = mybir.dt.float32
@@ -20,17 +18,24 @@ K = 1024
 FLOPS = 2 * B * CH * CH * K
 
 UNITS = 4 * B
-ROUNDS = 4 * B
+FRAMES = 4 * B
+RAW_BUFS = 8
+HEAD = [4, 5, 0, 1, 2, 3]
+HEAD_V_FROM = 4
+FIRST_FRAME_HALVES = 4
+EARLY_V = 3
+V_PATTERN = [1, 0, 0]
+SINGLE_FROM = 12
 
 
 def tile_guided_cam_module_pa_t_kernel(tc, x, query, out):
     nc = tc.nc
     with ExitStack() as ctx:
         const = ctx.enter_context(tc.tile_pool(name="const", bufs=1))
-        inp = ctx.enter_context(tc.tile_pool(name="inp", bufs=8))
+        inp = ctx.enter_context(tc.tile_pool(name="inp", bufs=RAW_BUFS))
         grp_pool = ctx.enter_context(tc.tile_pool(name="grp", bufs=3))
         code_pool = ctx.enter_context(tc.tile_pool(name="code", bufs=8))
-        e_pool = ctx.enter_context(tc.tile_pool(name="e", bufs=4))
+        e_pool = ctx.enter_context(tc.tile_pool(name="e", bufs=6))
         small = ctx.enter_context(tc.tile_pool(name="small", bufs=8))
         tps = ctx.enter_context(tc.psum_pool(name="tps", bufs=4))
         eps = ctx.enter_context(tc.psum_pool(name="eps", bufs=4))
@@ -38,107 +43,231 @@ def tile_guided_cam_module_pa_t_kernel(tc, x, query, out):
         ident = const.tile([P, P], F32)
         make_identity(nc, ident[:])
 
+        ctx.enter_context(tc.manual_schedule())
+
         raws = {}
+        alloc_order = []
+        transposed = set()
+        banks_of = {}
+        grps = {}
         codes = {}
         scales = {}
+        e_tiles = {}
+        e_banks = {}
+        mins = {}
+        sums = {}
+        recs = {}
 
-        def load(i):
-            b, u = divmod(i, 4)
-            a = u % 2
-            raw = inp.tile([P, 4096], BF16)
-            if u < 2:
+        def dram_unit(u):
+            b, q = divmod(u, 4)
+            if q < 2:
                 view = x[b].rearrange("(a p t) h w -> a p (t h w)", a=2, t=4)
             else:
                 view = query[b].rearrange("(p a t) h w -> a p (t h w)", a=2, t=4)
-            nc.sync.dma_start(out=raw[:], in_=view[a])
-            raws[i] = raw
+            return view[q % 2]
 
-        def prep(i):
-            rawf = raws[i][:].bitcast(F32)
-            grp = grp_pool.tile([P, 4096], BF16, align_bytes=64)
-            grpf = grp[:].bitcast(F32).rearrange("p (g c u) -> p g c u", g=2, u=2)
-            for t in range(4):
+        def raw_tile(u):
+            if u not in raws:
+                raw = inp.tile([P, 4096], BF16)
+                raws[u] = raw
+                alloc_order.append(u)
+            return raws[u]
+
+        def load_half(hf):
+            u, s = divmod(hf, 2)
+            raw = raw_tile(u)
+            nc.sync.dma_start(out=raw[:, s * 2048:(s + 1) * 2048],
+                              in_=dram_unit(u)[:, s * 2048:(s + 1) * 2048])
+
+        def load_unit(u):
+            raw = raw_tile(u)
+            nc.sync.dma_start(out=raw[:], in_=dram_unit(u))
+
+        def refill():
+            while len(alloc_order) < UNITS:
+                old = alloc_order[len(alloc_order) - RAW_BUFS]
+                if (2 * old) in transposed and (2 * old + 1) in transposed:
+                    load_unit(len(alloc_order))
+                else:
+                    break
+
+        def transposes(hf):
+            u, s = divmod(hf, 2)
+            rawf = raws[u][:].bitcast(F32)
+            banks_of[hf] = []
+            for t in (2 * s, 2 * s + 1):
                 tp = tps.tile([P, 4, P], F32)
                 for j in range(4):
                     lo = t * 512 + j * P
                     nc.tensor.transpose(tp[:, j, :], rawf[:, lo:lo + P], ident[:])
-                src = tp[:].rearrange("p (g u) c -> p g c u", u=2)
-                dst = grpf[:, :, t * P:(t + 1) * P, :]
-                on_vector = (t % 2 == 1) if i < 4 else (t == 3)
-                if on_vector:
-                    nc.vector.tensor_copy(out=dst, in_=src)
-                else:
-                    nc.scalar.copy(out=dst, in_=src)
-            cod = code_pool.tile([P, 1024], U32, align_bytes=64)
-            scl = code_pool.tile([P, 1024], U8, align_bytes=64)
-            nc.vector.quantize_mx(out=cod[:].bitcast(FP8X4), scales=scl[:], in_=grp[:])
-            codes[i] = cod
-            scales[i] = scl
+                banks_of[hf].append(tp)
+            transposed.add(hf)
 
-        def soft(j):
-            b, r = divmod(j, 4)
-            out_rows = out[b].rearrange("(p m) c -> p m c", m=8)
-            e_sb = e_pool.tile([P, 2, CH], F32)
-            for mi in range(2):
-                m = 2 * r + mi
-                qi = 4 * b + 2 + m // 4
-                t = m % 4
-                banks = []
-                for h in range(2):
-                    xi = 4 * b + h
-                    ep = eps.tile([P, 512], F32)
-                    for g in range(2):
-                        lo = g * 512 + t * P
-                        nc.tensor.matmul_mx(
-                            out=ep[:],
-                            lhsT=codes[qi][:, lo:lo + P].bitcast(FP8X4),
-                            lhsT_scale=scales[qi][:, lo:lo + P],
-                            rhs=codes[xi][:, g * 512:(g + 1) * 512].bitcast(FP8X4),
-                            rhs_scale=scales[xi][:, g * 512:(g + 1) * 512],
-                            start=(g == 0),
-                            stop=(g == 1),
-                        )
-                    banks.append(ep)
+        def copy_out(hf, k, on_vector):
+            u, s = divmod(hf, 2)
+            t = 2 * s + k
+            if u not in grps:
+                grp = grp_pool.tile([P, 4096], BF16, align_bytes=64)
+                grps[u] = grp
+            grpf = grps[u][:].bitcast(F32).rearrange("p (g c u) -> p g c u", g=2, u=2)
+            src = banks_of[hf][k][:].rearrange("p (g u) c -> p g c u", u=2)
+            dst = grpf[:, :, t * P:(t + 1) * P, :]
+            if on_vector:
+                nc.vector.tensor_copy(out=dst, in_=src)
+            else:
+                nc.scalar.copy(out=dst, in_=src)
+
+        def code_tiles(u):
+            if u not in codes:
+                cod = code_pool.tile([P, 1024], U32, align_bytes=64)
+                scl = code_pool.tile([P, 1024], U8, align_bytes=64)
+                codes[u] = cod
+                scales[u] = scl
+            return codes[u], scales[u]
+
+        def quant_half(hf):
+            u, s = divmod(hf, 2)
+            cod, scl = code_tiles(u)
+            for g in range(2):
+                w = g * 512 + s * 256
+                nc.vector.quantize_mx(out=cod[:, w:w + 256].bitcast(FP8X4),
+                                      scales=scl[:, w:w + 256],
+                                      in_=grps[u][:, 4 * w:4 * w + 1024])
+
+        def quant_unit(u):
+            cod, scl = code_tiles(u)
+            nc.vector.quantize_mx(out=cod[:].bitcast(FP8X4), scales=scl[:], in_=grps[u][:])
+
+        def energies(m):
+            b, mm = divmod(m, 8)
+            qi = 4 * b + 2 + mm // 4
+            t = mm % 4
+            e_banks[m] = []
+            for h in range(2):
+                xi = 4 * b + h
+                ep = eps.tile([P, 512], F32)
+                for g in range(2):
+                    lo = g * 512 + t * P
+                    nc.tensor.matmul_mx(
+                        out=ep[:],
+                        lhsT=codes[qi][:, lo:lo + P].bitcast(FP8X4),
+                        lhsT_scale=scales[qi][:, lo:lo + P],
+                        rhs=codes[xi][:, g * 512:(g + 1) * 512].bitcast(FP8X4),
+                        rhs_scale=scales[xi][:, g * 512:(g + 1) * 512],
+                        start=(g == 0),
+                        stop=(g == 1),
+                    )
+                e_banks[m].append(ep)
+
+        def row(m):
+            return e_tiles[m // 2][:, m % 2, :]
+
+        def min_pass(m, h):
+            if h == 0:
                 mn0 = small.tile([P, 1], F32)
+                mins[(m, 0)] = mn0
+                start_from = None
+            else:
                 mn = small.tile([P, 1], F32)
-                sm = small.tile([P, 1], F32)
-                rc = small.tile([P, 1], F32)
-                nc.vector.tensor_scalar(
-                    out=e_sb[:, mi, 0:512].rearrange("p (c t) -> p c t", t=4),
-                    in0=banks[0][:].rearrange("p (t c) -> p c t", t=4),
-                    scalar1=1.0, scalar2=None, op0=ALU.mult, op1=ALU.min,
-                    accum_out=mn0[:],
-                )
-                nc.vector.tensor_scalar(
-                    out=e_sb[:, mi, 512:1024].rearrange("p (c t) -> p c t", t=4),
-                    in0=banks[1][:].rearrange("p (t c) -> p c t", t=4),
-                    scalar1=1.0, scalar2=mn0[:], op0=ALU.mult, op1=ALU.min,
-                    accum_out=mn[:],
-                )
-                nc.scalar.activation(
-                    out=e_sb[:, mi, :], in_=e_sb[:, mi, :], func=ACT.Exp,
-                    bias=mn[:], scale=-1.0, accum_out=sm[:],
-                )
-                nc.vector.reciprocal(rc[:], sm[:])
-                nc.gpsimd.tensor_scalar(
-                    out=e_sb[:, mi, :], in0=e_sb[:, mi, :],
-                    scalar1=rc[:], scalar2=0.0, op0=ALU.mult, op1=ALU.add,
-                )
-            nc.sync.dma_start(out=out_rows[:, 2 * r:2 * r + 2, :], in_=e_sb[:])
+                mins[(m, 1)] = mn
+                start_from = mins[(m, 0)][:]
+            nc.vector.tensor_scalar(
+                out=row(m)[:, h * 512:(h + 1) * 512].rearrange("p (c t) -> p c t", t=4),
+                in0=e_banks[m][h][:].rearrange("p (t c) -> p c t", t=4),
+                scalar1=1.0, scalar2=start_from, op0=ALU.mult, op1=ALU.min,
+                accum_out=mins[(m, h)][:],
+            )
 
-        for i in range(8):
-            load(i)
+        def exponent(m):
+            sm = small.tile([P, 1], F32)
+            sums[m] = sm
+            nc.scalar.activation(out=row(m), in_=row(m), func=ACT.Exp,
+                                 bias=mins[(m, 1)][:], scale=-1.0, accum_out=sm[:])
 
-        def prep_and_refill(i):
-            if i < UNITS:
-                prep(i)
-                if i + 8 < UNITS:
-                    load(i + 8)
+        def reciprocal(m):
+            rc = small.tile([P, 1], F32)
+            recs[m] = rc
+            nc.vector.reciprocal(rc[:], sums[m][:])
 
-        for i in range(3):
-            prep_and_refill(i)
-        soft(0)
-        prep_and_refill(3)
-        for j in range(1, ROUNDS):
-            prep_and_refill(j + 3)
-            soft(j)
+        def normalise(m, on_vector):
+            if on_vector:
+                nc.vector.tensor_scalar(out=row(m), in0=row(m), scalar1=recs[m][:],
+                                        scalar2=None, op0=ALU.mult)
+            else:
+                nc.gpsimd.tensor_scalar(out=row(m), in0=row(m), scalar1=recs[m][:],
+                                        scalar2=0.0, op0=ALU.mult, op1=ALU.add)
+
+        def store_rows(m, n):
+            b, mm = divmod(m, 8)
+            out_rows = out[b].rearrange("(p m) c -> p m c", m=8)
+            nc.sync.dma_start(out=out_rows[:, mm:mm + n, :],
+                              in_=e_tiles[m // 2][:, m % 2:m % 2 + n, :])
+
+        for hf in HEAD:
+            load_half(hf)
+        for u in range(3, RAW_BUFS):
+            load_unit(u)
+
+        for n, hf in enumerate(HEAD):
+            transposes(hf)
+            copy_out(hf, 0, False)
+            copy_out(hf, 1, n >= HEAD_V_FROM)
+            if n > 0:
+                quant_half(HEAD[n - 1])
+        quant_half(HEAD[-1])
+        refill()
+
+        next_half = 6
+        previous = []
+        for j in range(FRAMES):
+            a = 2 * j
+            b2 = 2 * j + 1
+            count = FIRST_FRAME_HALVES if j == 0 else 2
+            halves = []
+            while len(halves) < count and next_half < 2 * UNITS:
+                halves.append(next_half)
+                next_half += 1
+            chunks = [halves[q:q + 2] for q in range(0, len(halves), 2)]
+            v_left = EARLY_V if len(halves) > 2 else V_PATTERN[j % len(V_PATTERN)]
+
+            e_pair = e_pool.tile([P, 2, CH], F32)
+            e_tiles[j] = e_pair
+            energies(a)
+            energies(b2)
+            if chunks:
+                for hf in chunks[0]:
+                    transposes(hf)
+                refill()
+            for m in (a, b2):
+                min_pass(m, 0)
+                if m >= 2:
+                    reciprocal(m - 2)
+                min_pass(m, 1)
+                exponent(m)
+            for hf in previous:
+                if hf % 2 == 1:
+                    quant_unit(hf // 2)
+            for n, chunk in enumerate(chunks):
+                if n > 0:
+                    for hf in chunk:
+                        transposes(hf)
+                    refill()
+                for hf in chunk:
+                    for k in range(2):
+                        copy_out(hf, k, v_left > 0)
+                        v_left -= 1
+            previous = halves
+            if j > 0:
+                normalise(a - 2, False)
+                if j - 1 >= SINGLE_FROM:
+                    store_rows(a - 2, 1)
+                normalise(a - 1, False)
+                if j - 1 >= SINGLE_FROM:
+                    store_rows(a - 1, 1)
+                else:
+                    store_rows(a - 2, 2)
+
+        for m in (2 * FRAMES - 2, 2 * FRAMES - 1):
+            reciprocal(m)
+            normalise(m, True)
+            store_rows(m, 1)

@@ -20,12 +20,10 @@ FLOPS = 2 * B * CH * CH * K
 UNITS = 4 * B
 FRAMES = 4 * B
 RAW_BUFS = 8
-HEAD = [4, 5, 0, 1, 2, 3]
-HEAD_V_FROM = 4
-FIRST_FRAME_HALVES = 4
-EARLY_V = 3
-V_PATTERN = [1, 0, 0]
-SINGLE_FROM = 12
+HEAD_UNITS = 5
+HALF_LOADS = 6
+V_COPIES = 1
+SINGLE_FROM = 11
 
 
 def tile_guided_cam_module_pa_t_kernel(tc, x, query, out):
@@ -179,22 +177,26 @@ def tile_guided_cam_module_pa_t_kernel(tc, x, query, out):
             )
 
         def exponent(m):
-            sm = small.tile([P, 1], F32)
-            sums[m] = sm
+            if m % 2 == 0:
+                sm = small.tile([P, 2], F32)
+                sums[m // 2] = sm
             nc.scalar.activation(out=row(m), in_=row(m), func=ACT.Exp,
-                                 bias=mins[(m, 1)][:], scale=-1.0, accum_out=sm[:])
+                                 bias=mins[(m, 1)][:], scale=-1.0,
+                                 accum_out=sums[m // 2][:, m % 2:m % 2 + 1])
 
-        def reciprocal(m):
-            rc = small.tile([P, 1], F32)
-            recs[m] = rc
-            nc.vector.reciprocal(rc[:], sums[m][:])
+        def reciprocal(m, n):
+            if m % 2 == 0:
+                rc = small.tile([P, 2], F32)
+                recs[m // 2] = rc
+            nc.vector.reciprocal(recs[m // 2][:, m % 2:m % 2 + n],
+                                 sums[m // 2][:, m % 2:m % 2 + n])
 
         def normalise(m, on_vector):
             if on_vector:
-                nc.vector.tensor_scalar(out=row(m), in0=row(m), scalar1=recs[m][:],
+                nc.vector.tensor_scalar(out=row(m), in0=row(m), scalar1=recs[m // 2][:, m % 2:m % 2 + 1],
                                         scalar2=None, op0=ALU.mult)
             else:
-                nc.gpsimd.tensor_scalar(out=row(m), in0=row(m), scalar1=recs[m][:],
+                nc.gpsimd.tensor_scalar(out=row(m), in0=row(m), scalar1=recs[m // 2][:, m % 2:m % 2 + 1],
                                         scalar2=0.0, op0=ALU.mult, op1=ALU.add)
 
         def store_rows(m, n):
@@ -203,71 +205,64 @@ def tile_guided_cam_module_pa_t_kernel(tc, x, query, out):
             nc.sync.dma_start(out=out_rows[:, mm:mm + n, :],
                               in_=e_tiles[m // 2][:, m % 2:m % 2 + n, :])
 
-        for hf in HEAD:
+        def finish(m):
+            normalise(m, False)
+            if m // 2 >= SINGLE_FROM:
+                store_rows(m, 1)
+            elif m % 2 == 1:
+                store_rows(m - 1, 2)
+
+        for hf in range(HALF_LOADS):
             load_half(hf)
-        for u in range(3, RAW_BUFS):
+        for u in range(HALF_LOADS // 2, RAW_BUFS):
             load_unit(u)
 
-        for n, hf in enumerate(HEAD):
+        for hf in range(2 * HEAD_UNITS):
             transposes(hf)
+            refill()
             copy_out(hf, 0, False)
-            copy_out(hf, 1, n >= HEAD_V_FROM)
-            if n > 0:
-                quant_half(HEAD[n - 1])
-        quant_half(HEAD[-1])
-        refill()
+            copy_out(hf, 1, False)
+            if hf > 0:
+                quant_half(hf - 1)
+        quant_half(2 * HEAD_UNITS - 1)
 
-        next_half = 6
-        previous = []
         for j in range(FRAMES):
             a = 2 * j
             b2 = 2 * j + 1
-            count = FIRST_FRAME_HALVES if j == 0 else 2
-            halves = []
-            while len(halves) < count and next_half < 2 * UNITS:
-                halves.append(next_half)
-                next_half += 1
-            chunks = [halves[q:q + 2] for q in range(0, len(halves), 2)]
-            v_left = EARLY_V if len(halves) > 2 else V_PATTERN[j % len(V_PATTERN)]
-
+            unit = j + HEAD_UNITS
             e_pair = e_pool.tile([P, 2, CH], F32)
             e_tiles[j] = e_pair
             energies(a)
             energies(b2)
-            if chunks:
-                for hf in chunks[0]:
-                    transposes(hf)
+            if unit < UNITS:
+                transposes(2 * unit)
+                transposes(2 * unit + 1)
                 refill()
-            for m in (a, b2):
-                min_pass(m, 0)
-                if m >= 2:
-                    reciprocal(m - 2)
-                min_pass(m, 1)
-                exponent(m)
-            for hf in previous:
-                if hf % 2 == 1:
-                    quant_unit(hf // 2)
-            for n, chunk in enumerate(chunks):
-                if n > 0:
-                    for hf in chunk:
-                        transposes(hf)
-                    refill()
-                for hf in chunk:
-                    for k in range(2):
-                        copy_out(hf, k, v_left > 0)
-                        v_left -= 1
-            previous = halves
-            if j > 0:
-                normalise(a - 2, False)
-                if j - 1 >= SINGLE_FROM:
-                    store_rows(a - 2, 1)
-                normalise(a - 1, False)
-                if j - 1 >= SINGLE_FROM:
-                    store_rows(a - 1, 1)
-                else:
-                    store_rows(a - 2, 2)
+            if unit <= UNITS:
+                if j > 0:
+                    reciprocal(a - 2, 2)
+                    finish(a - 2)
+                    finish(a - 1)
+                for m in (a, b2):
+                    min_pass(m, 0)
+                    min_pass(m, 1)
+                    exponent(m)
+                banks = [(2 * unit + s, k) for s in range(2) for k in range(2)] if unit < UNITS else []
+                for hf, k in banks[:V_COPIES]:
+                    copy_out(hf, k, True)
+                if j > 0:
+                    quant_unit(unit - 1)
+                for hf, k in banks[V_COPIES:]:
+                    copy_out(hf, k, False)
+            else:
+                for m in (a, b2):
+                    min_pass(m, 0)
+                    reciprocal(m - 2, 1)
+                    finish(m - 2)
+                    min_pass(m, 1)
+                    exponent(m)
 
         for m in (2 * FRAMES - 2, 2 * FRAMES - 1):
-            reciprocal(m)
+            reciprocal(m, 1)
             normalise(m, True)
             store_rows(m, 1)

@@ -56,12 +56,12 @@ def tile_guided_cam_module_pa_t_kernel(tc, x, query, out):
         sums = {}
         recs = {}
 
-        def dram_unit(u):
+        def dram_halves(u):
             b, q = divmod(u, 4)
             if q < 2:
-                view = x[b].rearrange("(a p t) h w -> a p (t h w)", a=2, t=4)
+                view = x[b].rearrange("(u a p t) h w -> u a p (t h w)", u=2, a=2, t=2)
             else:
-                view = query[b].rearrange("(p a t) h w -> a p (t h w)", a=2, t=4)
+                view = query[b].rearrange("(p u a t) h w -> u a p (t h w)", u=2, a=2, t=2)
             return view[q % 2]
 
         def raw_tile(u):
@@ -75,11 +75,12 @@ def tile_guided_cam_module_pa_t_kernel(tc, x, query, out):
             u, s = divmod(hf, 2)
             raw = raw_tile(u)
             nc.sync.dma_start(out=raw[:, s * 2048:(s + 1) * 2048],
-                              in_=dram_unit(u)[:, s * 2048:(s + 1) * 2048])
+                              in_=dram_halves(u)[s])
 
         def load_unit(u):
             raw = raw_tile(u)
-            nc.sync.dma_start(out=raw[:], in_=dram_unit(u))
+            nc.sync.dma_start(out=raw[:].rearrange("p (a k) -> p a k", a=2),
+                              in_=dram_halves(u).rearrange("a p k -> p a k"))
 
         def refill():
             while len(alloc_order) < UNITS:
@@ -170,8 +171,8 @@ def tile_guided_cam_module_pa_t_kernel(tc, x, query, out):
                 mins[(m, 1)] = mn
                 start_from = mins[(m, 0)][:]
             nc.vector.tensor_scalar(
-                out=row(m)[:, h * 512:(h + 1) * 512].rearrange("p (c t) -> p c t", t=4),
-                in0=e_banks[m][h][:].rearrange("p (t c) -> p c t", t=4),
+                out=row(m)[:, h * 512:(h + 1) * 512].rearrange("p (a c t) -> p a c t", a=2, t=2),
+                in0=e_banks[m][h][:].rearrange("p (a t c) -> p a c t", a=2, t=2),
                 scalar1=1.0, scalar2=start_from, op0=ALU.mult, op1=ALU.min,
                 accum_out=mins[(m, h)][:],
             )

@@ -41,8 +41,6 @@ def tile_guided_cam_module_pa_t_kernel(tc, x, query, out):
         ident = const.tile([P, P], F32)
         make_identity(nc, ident[:])
 
-        ctx.enter_context(tc.manual_schedule())
-
         raws = {}
         alloc_order = []
         transposed = set()
@@ -56,12 +54,12 @@ def tile_guided_cam_module_pa_t_kernel(tc, x, query, out):
         sums = {}
         recs = {}
 
-        def dram_halves(u):
+        def dram_unit(u):
             b, q = divmod(u, 4)
             if q < 2:
-                view = x[b].rearrange("(u a p t) h w -> u a p (t h w)", u=2, a=2, t=2)
+                view = x[b].rearrange("(a p t) h w -> a p (t h w)", a=2, t=4)
             else:
-                view = query[b].rearrange("(p u a t) h w -> u a p (t h w)", u=2, a=2, t=2)
+                view = query[b].rearrange("(p a t) h w -> a p (t h w)", a=2, t=4)
             return view[q % 2]
 
         def raw_tile(u):
@@ -75,12 +73,11 @@ def tile_guided_cam_module_pa_t_kernel(tc, x, query, out):
             u, s = divmod(hf, 2)
             raw = raw_tile(u)
             nc.sync.dma_start(out=raw[:, s * 2048:(s + 1) * 2048],
-                              in_=dram_halves(u)[s])
+                              in_=dram_unit(u)[:, s * 2048:(s + 1) * 2048])
 
         def load_unit(u):
             raw = raw_tile(u)
-            nc.sync.dma_start(out=raw[:].rearrange("p (a k) -> p a k", a=2),
-                              in_=dram_halves(u).rearrange("a p k -> p a k"))
+            nc.sync.dma_start(out=raw[:], in_=dram_unit(u))
 
         def refill():
             while len(alloc_order) < UNITS:
@@ -171,8 +168,8 @@ def tile_guided_cam_module_pa_t_kernel(tc, x, query, out):
                 mins[(m, 1)] = mn
                 start_from = mins[(m, 0)][:]
             nc.vector.tensor_scalar(
-                out=row(m)[:, h * 512:(h + 1) * 512].rearrange("p (a c t) -> p a c t", a=2, t=2),
-                in0=e_banks[m][h][:].rearrange("p (a t c) -> p a c t", a=2, t=2),
+                out=row(m)[:, h * 512:(h + 1) * 512].rearrange("p (c t) -> p c t", t=4),
+                in0=e_banks[m][h][:].rearrange("p (t c) -> p c t", t=4),
                 scalar1=1.0, scalar2=start_from, op0=ALU.mult, op1=ALU.min,
                 accum_out=mins[(m, h)][:],
             )

@@ -17,13 +17,17 @@ CH = 1024
 K = 1024
 FLOPS = 2 * B * CH * CH * K
 
+BANK = 512
+UNIT_COLS = 4 * K
 UNITS = 4 * B
 FRAMES = 4 * B
-RAW_BUFS = 8
+ROW_TILES = 2 * FRAMES
+
 HEAD_UNITS = 5
-HALF_LOADS = 6
-V_COPIES = 1
-SINGLE_FROM = 11
+HALF_LOADS = 2 * HEAD_UNITS
+RAW_BUFS = 8
+VECTOR_COPIES = 1
+SINGLE_STORES_FROM = UNITS - HEAD_UNITS
 
 
 def tile_guided_cam_module_pa_t_kernel(tc, x, query, out):
@@ -41,9 +45,9 @@ def tile_guided_cam_module_pa_t_kernel(tc, x, query, out):
         ident = const.tile([P, P], F32)
         make_identity(nc, ident[:])
 
+        ctx.enter_context(tc.manual_schedule())
+
         raws = {}
-        alloc_order = []
-        transposed = set()
         banks_of = {}
         grps = {}
         codes = {}
@@ -64,50 +68,40 @@ def tile_guided_cam_module_pa_t_kernel(tc, x, query, out):
 
         def raw_tile(u):
             if u not in raws:
-                raw = inp.tile([P, 4096], BF16)
+                raw = inp.tile([P, UNIT_COLS], BF16)
                 raws[u] = raw
-                alloc_order.append(u)
             return raws[u]
 
         def load_half(hf):
             u, s = divmod(hf, 2)
-            raw = raw_tile(u)
-            nc.sync.dma_start(out=raw[:, s * 2048:(s + 1) * 2048],
-                              in_=dram_unit(u)[:, s * 2048:(s + 1) * 2048])
+            cols = slice(s * 2 * K, (s + 1) * 2 * K)
+            nc.sync.dma_start(out=raw_tile(u)[:, cols], in_=dram_unit(u)[:, cols])
 
         def load_unit(u):
-            raw = raw_tile(u)
-            nc.sync.dma_start(out=raw[:], in_=dram_unit(u))
-
-        def refill():
-            while len(alloc_order) < UNITS:
-                old = alloc_order[len(alloc_order) - RAW_BUFS]
-                if (2 * old) in transposed and (2 * old + 1) in transposed:
-                    load_unit(len(alloc_order))
-                else:
-                    break
+            nc.sync.dma_start(out=raw_tile(u)[:], in_=dram_unit(u))
 
         def transposes(hf):
             u, s = divmod(hf, 2)
-            rawf = raws[u][:].bitcast(F32)
+            words = raws[u][:].bitcast(F32)
             banks_of[hf] = []
             for t in (2 * s, 2 * s + 1):
                 tp = tps.tile([P, 4, P], F32)
-                for j in range(4):
-                    lo = t * 512 + j * P
-                    nc.tensor.transpose(tp[:, j, :], rawf[:, lo:lo + P], ident[:])
+                for plane in range(4):
+                    lo = t * (K // 2) + plane * P
+                    nc.tensor.transpose(tp[:, plane, :], words[:, lo:lo + P], ident[:])
                 banks_of[hf].append(tp)
-            transposed.add(hf)
+            if s == 1 and u + RAW_BUFS < UNITS:
+                load_unit(u + RAW_BUFS)
 
-        def copy_out(hf, k, on_vector):
+        def copy_out(hf, i, on_vector):
             u, s = divmod(hf, 2)
-            t = 2 * s + k
+            t = 2 * s + i
             if u not in grps:
-                grp = grp_pool.tile([P, 4096], BF16, align_bytes=64)
+                grp = grp_pool.tile([P, UNIT_COLS], BF16, align_bytes=64)
                 grps[u] = grp
-            grpf = grps[u][:].bitcast(F32).rearrange("p (g c u) -> p g c u", g=2, u=2)
-            src = banks_of[hf][k][:].rearrange("p (g u) c -> p g c u", u=2)
-            dst = grpf[:, :, t * P:(t + 1) * P, :]
+            grouped = grps[u][:].bitcast(F32).rearrange("p (g c w) -> p g c w", g=2, w=2)
+            src = banks_of[hf][i][:].rearrange("p (g w) c -> p g c w", w=2)
+            dst = grouped[:, :, t * P:(t + 1) * P, :]
             if on_vector:
                 nc.vector.tensor_copy(out=dst, in_=src)
             else:
@@ -115,8 +109,8 @@ def tile_guided_cam_module_pa_t_kernel(tc, x, query, out):
 
         def code_tiles(u):
             if u not in codes:
-                cod = code_pool.tile([P, 1024], U32, align_bytes=64)
-                scl = code_pool.tile([P, 1024], U8, align_bytes=64)
+                cod = code_pool.tile([P, 2 * BANK], U32, align_bytes=64)
+                scl = code_pool.tile([P, 2 * BANK], U8, align_bytes=64)
                 codes[u] = cod
                 scales[u] = scl
             return codes[u], scales[u]
@@ -125,10 +119,10 @@ def tile_guided_cam_module_pa_t_kernel(tc, x, query, out):
             u, s = divmod(hf, 2)
             cod, scl = code_tiles(u)
             for g in range(2):
-                w = g * 512 + s * 256
-                nc.vector.quantize_mx(out=cod[:, w:w + 256].bitcast(FP8X4),
-                                      scales=scl[:, w:w + 256],
-                                      in_=grps[u][:, 4 * w:4 * w + 1024])
+                w = g * BANK + s * 2 * P
+                nc.vector.quantize_mx(out=cod[:, w:w + 2 * P].bitcast(FP8X4),
+                                      scales=scl[:, w:w + 2 * P],
+                                      in_=grps[u][:, 4 * w:4 * (w + 2 * P)])
 
         def quant_unit(u):
             cod, scl = code_tiles(u)
@@ -136,20 +130,20 @@ def tile_guided_cam_module_pa_t_kernel(tc, x, query, out):
 
         def energies(m):
             b, mm = divmod(m, 8)
-            qi = 4 * b + 2 + mm // 4
+            qu = 4 * b + 2 + mm // 4
             t = mm % 4
             e_banks[m] = []
             for h in range(2):
-                xi = 4 * b + h
-                ep = eps.tile([P, 512], F32)
+                xu = 4 * b + h
+                ep = eps.tile([P, BANK], F32)
                 for g in range(2):
-                    lo = g * 512 + t * P
+                    lo = g * BANK + t * P
                     nc.tensor.matmul_mx(
                         out=ep[:],
-                        lhsT=codes[qi][:, lo:lo + P].bitcast(FP8X4),
-                        lhsT_scale=scales[qi][:, lo:lo + P],
-                        rhs=codes[xi][:, g * 512:(g + 1) * 512].bitcast(FP8X4),
-                        rhs_scale=scales[xi][:, g * 512:(g + 1) * 512],
+                        lhsT=codes[qu][:, lo:lo + P].bitcast(FP8X4),
+                        lhsT_scale=scales[qu][:, lo:lo + P],
+                        rhs=codes[xu][:, g * BANK:(g + 1) * BANK].bitcast(FP8X4),
+                        rhs_scale=scales[xu][:, g * BANK:(g + 1) * BANK],
                         start=(g == 0),
                         stop=(g == 1),
                     )
@@ -168,7 +162,7 @@ def tile_guided_cam_module_pa_t_kernel(tc, x, query, out):
                 mins[(m, 1)] = mn
                 start_from = mins[(m, 0)][:]
             nc.vector.tensor_scalar(
-                out=row(m)[:, h * 512:(h + 1) * 512].rearrange("p (c t) -> p c t", t=4),
+                out=row(m)[:, h * BANK:(h + 1) * BANK].rearrange("p (c t) -> p c t", t=4),
                 in0=e_banks[m][h][:].rearrange("p (t c) -> p c t", t=4),
                 scalar1=1.0, scalar2=start_from, op0=ALU.mult, op1=ALU.min,
                 accum_out=mins[(m, h)][:],
@@ -190,11 +184,12 @@ def tile_guided_cam_module_pa_t_kernel(tc, x, query, out):
                                  sums[m // 2][:, m % 2:m % 2 + n])
 
         def normalise(m, on_vector):
+            factor = recs[m // 2][:, m % 2:m % 2 + 1]
             if on_vector:
-                nc.vector.tensor_scalar(out=row(m), in0=row(m), scalar1=recs[m // 2][:, m % 2:m % 2 + 1],
+                nc.vector.tensor_scalar(out=row(m), in0=row(m), scalar1=factor,
                                         scalar2=None, op0=ALU.mult)
             else:
-                nc.gpsimd.tensor_scalar(out=row(m), in0=row(m), scalar1=recs[m // 2][:, m % 2:m % 2 + 1],
+                nc.gpsimd.tensor_scalar(out=row(m), in0=row(m), scalar1=factor,
                                         scalar2=0.0, op0=ALU.mult, op1=ALU.add)
 
         def store_rows(m, n):
@@ -205,7 +200,7 @@ def tile_guided_cam_module_pa_t_kernel(tc, x, query, out):
 
         def finish(m):
             normalise(m, False)
-            if m // 2 >= SINGLE_FROM:
+            if m // 2 >= SINGLE_STORES_FROM:
                 store_rows(m, 1)
             elif m % 2 == 1:
                 store_rows(m - 1, 2)
@@ -217,7 +212,6 @@ def tile_guided_cam_module_pa_t_kernel(tc, x, query, out):
 
         for hf in range(2 * HEAD_UNITS):
             transposes(hf)
-            refill()
             copy_out(hf, 0, False)
             copy_out(hf, 1, False)
             if hf > 0:
@@ -225,42 +219,41 @@ def tile_guided_cam_module_pa_t_kernel(tc, x, query, out):
         quant_half(2 * HEAD_UNITS - 1)
 
         for j in range(FRAMES):
-            a = 2 * j
-            b2 = 2 * j + 1
+            first = 2 * j
+            second = 2 * j + 1
             unit = j + HEAD_UNITS
             e_pair = e_pool.tile([P, 2, CH], F32)
             e_tiles[j] = e_pair
-            energies(a)
-            energies(b2)
+            energies(first)
+            energies(second)
             if unit < UNITS:
                 transposes(2 * unit)
                 transposes(2 * unit + 1)
-                refill()
             if unit <= UNITS:
                 if j > 0:
-                    reciprocal(a - 2, 2)
-                    finish(a - 2)
-                    finish(a - 1)
-                for m in (a, b2):
+                    reciprocal(first - 2, 2)
+                    finish(first - 2)
+                    finish(first - 1)
+                for m in (first, second):
                     min_pass(m, 0)
                     min_pass(m, 1)
                     exponent(m)
-                banks = [(2 * unit + s, k) for s in range(2) for k in range(2)] if unit < UNITS else []
-                for hf, k in banks[:V_COPIES]:
-                    copy_out(hf, k, True)
+                banks = [(2 * unit + s, i) for s in range(2) for i in range(2)] if unit < UNITS else []
+                for hf, i in banks[:VECTOR_COPIES]:
+                    copy_out(hf, i, True)
                 if j > 0:
                     quant_unit(unit - 1)
-                for hf, k in banks[V_COPIES:]:
-                    copy_out(hf, k, False)
+                for hf, i in banks[VECTOR_COPIES:]:
+                    copy_out(hf, i, False)
             else:
-                for m in (a, b2):
+                for m in (first, second):
                     min_pass(m, 0)
                     reciprocal(m - 2, 1)
                     finish(m - 2)
                     min_pass(m, 1)
                     exponent(m)
 
-        for m in (2 * FRAMES - 2, 2 * FRAMES - 1):
+        for m in (ROW_TILES - 2, ROW_TILES - 1):
             reciprocal(m, 1)
             normalise(m, True)
             store_rows(m, 1)

@@ -128,26 +128,24 @@ def tile_guided_cam_module_pa_t_kernel(tc, x, query, out):
             cod, scl = code_tiles(u)
             nc.vector.quantize_mx(out=cod[:].bitcast(FP8X4), scales=scl[:], in_=grps[u][:])
 
-        def energies(m):
+        def energies(m, h):
             b, mm = divmod(m, 8)
             qu = 4 * b + 2 + mm // 4
             t = mm % 4
-            e_banks[m] = []
-            for h in range(2):
-                xu = 4 * b + h
-                ep = eps.tile([P, BANK], F32)
-                for g in range(2):
-                    lo = g * BANK + t * P
-                    nc.tensor.matmul_mx(
-                        out=ep[:],
-                        lhsT=codes[qu][:, lo:lo + P].bitcast(FP8X4),
-                        lhsT_scale=scales[qu][:, lo:lo + P],
-                        rhs=codes[xu][:, g * BANK:(g + 1) * BANK].bitcast(FP8X4),
-                        rhs_scale=scales[xu][:, g * BANK:(g + 1) * BANK],
-                        start=(g == 0),
-                        stop=(g == 1),
-                    )
-                e_banks[m].append(ep)
+            xu = 4 * b + h
+            ep = eps.tile([P, BANK], F32)
+            for g in range(2):
+                lo = g * BANK + t * P
+                nc.tensor.matmul_mx(
+                    out=ep[:],
+                    lhsT=codes[qu][:, lo:lo + P].bitcast(FP8X4),
+                    lhsT_scale=scales[qu][:, lo:lo + P],
+                    rhs=codes[xu][:, g * BANK:(g + 1) * BANK].bitcast(FP8X4),
+                    rhs_scale=scales[xu][:, g * BANK:(g + 1) * BANK],
+                    start=(g == 0),
+                    stop=(g == 1),
+                )
+            e_banks[(m, h)] = ep
 
         def row(m):
             return e_tiles[m // 2][:, m % 2, :]
@@ -163,7 +161,7 @@ def tile_guided_cam_module_pa_t_kernel(tc, x, query, out):
                 start_from = mins[(m, 0)][:]
             nc.vector.tensor_scalar(
                 out=row(m)[:, h * BANK:(h + 1) * BANK].rearrange("p (c t) -> p c t", t=4),
-                in0=e_banks[m][h][:].rearrange("p (t c) -> p c t", t=4),
+                in0=e_banks[(m, h)][:].rearrange("p (t c) -> p c t", t=4),
                 scalar1=1.0, scalar2=start_from, op0=ALU.mult, op1=ALU.min,
                 accum_out=mins[(m, h)][:],
             )
@@ -224,8 +222,9 @@ def tile_guided_cam_module_pa_t_kernel(tc, x, query, out):
             unit = j + HEAD_UNITS
             e_pair = e_pool.tile([P, 2, CH], F32)
             e_tiles[j] = e_pair
-            energies(first)
-            energies(second)
+            for h in range(2):
+                energies(first, h)
+                energies(second, h)
             if unit < UNITS:
                 transposes(2 * unit)
                 transposes(2 * unit + 1)
@@ -234,10 +233,12 @@ def tile_guided_cam_module_pa_t_kernel(tc, x, query, out):
                     reciprocal(first - 2, 2)
                     finish(first - 2)
                     finish(first - 1)
-                for m in (first, second):
-                    min_pass(m, 0)
-                    min_pass(m, 1)
-                    exponent(m)
+                min_pass(first, 0)
+                min_pass(second, 0)
+                min_pass(first, 1)
+                exponent(first)
+                min_pass(second, 1)
+                exponent(second)
                 banks = [(2 * unit + s, i) for s in range(2) for i in range(2)] if unit < UNITS else []
                 for hf, i in banks[:VECTOR_COPIES]:
                     copy_out(hf, i, True)
@@ -246,12 +247,16 @@ def tile_guided_cam_module_pa_t_kernel(tc, x, query, out):
                 for hf, i in banks[VECTOR_COPIES:]:
                     copy_out(hf, i, False)
             else:
-                for m in (first, second):
-                    min_pass(m, 0)
-                    reciprocal(m - 2, 1)
-                    finish(m - 2)
-                    min_pass(m, 1)
-                    exponent(m)
+                min_pass(first, 0)
+                reciprocal(first - 2, 1)
+                finish(first - 2)
+                min_pass(second, 0)
+                min_pass(first, 1)
+                exponent(first)
+                reciprocal(second - 2, 1)
+                finish(second - 2)
+                min_pass(second, 1)
+                exponent(second)
 
         for m in (ROW_TILES - 2, ROW_TILES - 1):
             reciprocal(m, 1)

@@ -23,8 +23,10 @@ UNITS = 4 * B
 FRAMES = 4 * B
 ROW_TILES = 2 * FRAMES
 
-HEAD_UNITS = 5
-HALF_LOADS = 2 * HEAD_UNITS
+HEAD_UNITS = 4
+HEAD_HALVES = (0, 2, 3, 4, 5, 1, 6, 7)
+FRAME_0_AT = 7
+HALF_UNITS = 3
 RAW_BUFS = 8
 VECTOR_COPIES = 1
 SINGLE_STORES_FROM = UNITS - HEAD_UNITS
@@ -35,7 +37,7 @@ def tile_guided_cam_module_pa_t_kernel(tc, x, query, out):
     with ExitStack() as ctx:
         const = ctx.enter_context(tc.tile_pool(name="const", bufs=1))
         inp = ctx.enter_context(tc.tile_pool(name="inp", bufs=RAW_BUFS))
-        grp_pool = ctx.enter_context(tc.tile_pool(name="grp", bufs=3))
+        grp_pool = ctx.enter_context(tc.tile_pool(name="grp", bufs=4))
         code_pool = ctx.enter_context(tc.tile_pool(name="code", bufs=8))
         e_pool = ctx.enter_context(tc.tile_pool(name="e", bufs=6))
         small = ctx.enter_context(tc.tile_pool(name="small", bufs=8))
@@ -60,11 +62,9 @@ def tile_guided_cam_module_pa_t_kernel(tc, x, query, out):
 
         def dram_unit(u):
             b, q = divmod(u, 4)
-            if q < 2:
-                view = x[b].rearrange("(a p t) h w -> a p (t h w)", a=2, t=4)
-            else:
-                view = query[b].rearrange("(p a t) h w -> a p (t h w)", a=2, t=4)
-            return view[q % 2]
+            if q in (1, 2):
+                return x[b].rearrange("(a p t) h w -> a p (t h w)", a=2, t=4)[q - 1]
+            return query[b].rearrange("(p a t) h w -> a p (t h w)", a=2, t=4)[q // 3]
 
         def raw_tile(u):
             if u not in raws:
@@ -90,8 +90,6 @@ def tile_guided_cam_module_pa_t_kernel(tc, x, query, out):
                     lo = t * (K // 2) + plane * P
                     nc.tensor.transpose(tp[:, plane, :], words[:, lo:lo + P], ident[:])
                 banks_of[hf].append(tp)
-            if s == 1 and u + RAW_BUFS < UNITS:
-                load_unit(u + RAW_BUFS)
 
         def copy_out(hf, i, on_vector):
             u, s = divmod(hf, 2)
@@ -99,9 +97,14 @@ def tile_guided_cam_module_pa_t_kernel(tc, x, query, out):
             if u not in grps:
                 grp = grp_pool.tile([P, UNIT_COLS], BF16, align_bytes=64)
                 grps[u] = grp
-            grouped = grps[u][:].bitcast(F32).rearrange("p (g c w) -> p g c w", g=2, w=2)
+            words = grps[u][:].bitcast(F32)
             src = banks_of[hf][i][:].rearrange("p (g w) c -> p g c w", w=2)
-            dst = grouped[:, :, t * P:(t + 1) * P, :]
+            if u < HALF_UNITS:
+                grouped = words.rearrange("p (s g c w) -> p s g c w", s=2, g=2, w=2)
+                dst = grouped[:, s, :, i * P:(i + 1) * P, :]
+            else:
+                grouped = words.rearrange("p (g c w) -> p g c w", g=2, w=2)
+                dst = grouped[:, :, t * P:(t + 1) * P, :]
             if on_vector:
                 nc.vector.tensor_copy(out=dst, in_=src)
             else:
@@ -120,9 +123,10 @@ def tile_guided_cam_module_pa_t_kernel(tc, x, query, out):
             cod, scl = code_tiles(u)
             for g in range(2):
                 w = g * BANK + s * 2 * P
+                lo = 4 * (s * BANK + g * 2 * P)
                 nc.vector.quantize_mx(out=cod[:, w:w + 2 * P].bitcast(FP8X4),
                                       scales=scl[:, w:w + 2 * P],
-                                      in_=grps[u][:, 4 * w:4 * (w + 2 * P)])
+                                      in_=grps[u][:, lo:lo + 4 * 2 * P])
 
         def quant_unit(u):
             cod, scl = code_tiles(u)
@@ -130,9 +134,9 @@ def tile_guided_cam_module_pa_t_kernel(tc, x, query, out):
 
         def energies(m, h):
             b, mm = divmod(m, 8)
-            qu = 4 * b + 2 + mm // 4
+            qu = 4 * b + 3 * (mm // 4)
             t = mm % 4
-            xu = 4 * b + h
+            xu = 4 * b + 1 + h
             ep = eps.tile([P, BANK], F32)
             for g in range(2):
                 lo = g * BANK + t * P
@@ -146,6 +150,11 @@ def tile_guided_cam_module_pa_t_kernel(tc, x, query, out):
                     stop=(g == 1),
                 )
             e_banks[(m, h)] = ep
+
+        def frame_energies(j):
+            for h in range(2):
+                energies(2 * j, h)
+                energies(2 * j + 1, h)
 
         def row(m):
             return e_tiles[m // 2][:, m % 2, :]
@@ -203,18 +212,21 @@ def tile_guided_cam_module_pa_t_kernel(tc, x, query, out):
             elif m % 2 == 1:
                 store_rows(m - 1, 2)
 
-        for hf in range(HALF_LOADS):
+        for hf in HEAD_HALVES:
             load_half(hf)
-        for u in range(HALF_LOADS // 2, RAW_BUFS):
+        for u in range(HEAD_UNITS, RAW_BUFS):
             load_unit(u)
 
-        for hf in range(2 * HEAD_UNITS):
+        for n, hf in enumerate(HEAD_HALVES):
+            if n == FRAME_0_AT:
+                frame_energies(0)
             transposes(hf)
+            if 0 < n < FRAME_0_AT:
+                quant_half(HEAD_HALVES[n - 1])
             copy_out(hf, 0, False)
             copy_out(hf, 1, False)
-            if hf > 0:
-                quant_half(hf - 1)
-        quant_half(2 * HEAD_UNITS - 1)
+        for u in range(RAW_BUFS, RAW_BUFS + HEAD_UNITS):
+            load_unit(u)
 
         for j in range(FRAMES):
             first = 2 * j
@@ -222,12 +234,13 @@ def tile_guided_cam_module_pa_t_kernel(tc, x, query, out):
             unit = j + HEAD_UNITS
             e_pair = e_pool.tile([P, 2, CH], F32)
             e_tiles[j] = e_pair
-            for h in range(2):
-                energies(first, h)
-                energies(second, h)
+            if j > 0:
+                frame_energies(j)
             if unit < UNITS:
                 transposes(2 * unit)
                 transposes(2 * unit + 1)
+                if unit + RAW_BUFS < UNITS:
+                    load_unit(unit + RAW_BUFS)
             if unit <= UNITS:
                 if j > 0:
                     reciprocal(first - 2, 2)
@@ -242,8 +255,7 @@ def tile_guided_cam_module_pa_t_kernel(tc, x, query, out):
                 banks = [(2 * unit + s, i) for s in range(2) for i in range(2)] if unit < UNITS else []
                 for hf, i in banks[:VECTOR_COPIES]:
                     copy_out(hf, i, True)
-                if j > 0:
-                    quant_unit(unit - 1)
+                quant_unit(unit - 1)
                 for hf, i in banks[VECTOR_COPIES:]:
                     copy_out(hf, i, False)
             else:

@@ -28,7 +28,7 @@ HEAD_HALVES = (0, 2, 3, 4, 5, 1, 6, 7)
 FRAME_0_AT = 7
 HALF_UNITS = 3
 RAW_BUFS = 8
-VECTOR_COPIES = 1
+VECTOR_COPIES = (1, 1, 0)
 SINGLE_STORES_FROM = UNITS - HEAD_UNITS
 
 
@@ -39,7 +39,7 @@ def tile_guided_cam_module_pa_t_kernel(tc, x, query, out):
         inp = ctx.enter_context(tc.tile_pool(name="inp", bufs=RAW_BUFS))
         grp_pool = ctx.enter_context(tc.tile_pool(name="grp", bufs=4))
         code_pool = ctx.enter_context(tc.tile_pool(name="code", bufs=8))
-        e_pool = ctx.enter_context(tc.tile_pool(name="e", bufs=6))
+        e_pool = ctx.enter_context(tc.tile_pool(name="e", bufs=7))
         small = ctx.enter_context(tc.tile_pool(name="small", bufs=8))
         tps = ctx.enter_context(tc.psum_pool(name="tps", bufs=4))
         eps = ctx.enter_context(tc.psum_pool(name="eps", bufs=4))
@@ -242,10 +242,10 @@ def tile_guided_cam_module_pa_t_kernel(tc, x, query, out):
                 if unit + RAW_BUFS < UNITS:
                     load_unit(unit + RAW_BUFS)
             if unit <= UNITS:
-                if j > 0:
-                    reciprocal(first - 2, 2)
-                    finish(first - 2)
-                    finish(first - 1)
+                if j > 1:
+                    reciprocal(first - 4, 2)
+                    finish(first - 4)
+                    finish(first - 3)
                 min_pass(first, 0)
                 min_pass(second, 0)
                 min_pass(first, 1)
@@ -253,12 +253,17 @@ def tile_guided_cam_module_pa_t_kernel(tc, x, query, out):
                 min_pass(second, 1)
                 exponent(second)
                 banks = [(2 * unit + s, i) for s in range(2) for i in range(2)] if unit < UNITS else []
-                for hf, i in banks[:VECTOR_COPIES]:
+                vector_copies = VECTOR_COPIES[j % len(VECTOR_COPIES)]
+                for hf, i in banks[:vector_copies]:
                     copy_out(hf, i, True)
                 quant_unit(unit - 1)
-                for hf, i in banks[VECTOR_COPIES:]:
+                for hf, i in banks[vector_copies:]:
                     copy_out(hf, i, False)
             else:
+                if unit == UNITS + 1:
+                    reciprocal(first - 4, 2)
+                    finish(first - 4)
+                    finish(first - 3)
                 min_pass(first, 0)
                 reciprocal(first - 2, 1)
                 finish(first - 2)

@@ -25,7 +25,7 @@ ROW_TILES = 2 * FRAMES
 
 HEAD_UNITS = 4
 HEAD_HALVES = (0, 2, 3, 4, 5, 1, 6, 7)
-FRAME_0_AT = 7
+FRAME_0_AT = (5, 7)
 HALF_UNITS = 3
 RAW_BUFS = 8
 VECTOR_COPIES = (1, 1, 0)
@@ -151,10 +151,13 @@ def tile_guided_cam_module_pa_t_kernel(tc, x, query, out):
                 )
             e_banks[(m, h)] = ep
 
+        def half_energies(j, h):
+            energies(2 * j, h)
+            energies(2 * j + 1, h)
+
         def frame_energies(j):
             for h in range(2):
-                energies(2 * j, h)
-                energies(2 * j + 1, h)
+                half_energies(j, h)
 
         def row(m):
             return e_tiles[m // 2][:, m % 2, :]
@@ -175,23 +178,34 @@ def tile_guided_cam_module_pa_t_kernel(tc, x, query, out):
                 accum_out=mins[(m, h)][:],
             )
 
+        def first_passes(j):
+            e_pair = e_pool.tile([P, 2, CH], F32)
+            e_tiles[j] = e_pair
+            min_pass(2 * j, 0)
+            min_pass(2 * j + 1, 0)
+
+        def pair_column(m):
+            return divmod(m + 1, 2)
+
         def exponent(m):
-            if m % 2 == 0:
+            q, col = pair_column(m)
+            if q not in sums:
                 sm = small.tile([P, 2], F32)
-                sums[m // 2] = sm
+                sums[q] = sm
             nc.scalar.activation(out=row(m), in_=row(m), func=ACT.Exp,
                                  bias=mins[(m, 1)][:], scale=-1.0,
-                                 accum_out=sums[m // 2][:, m % 2:m % 2 + 1])
+                                 accum_out=sums[q][:, col:col + 1])
 
         def reciprocal(m, n):
-            if m % 2 == 0:
+            q, col = pair_column(m)
+            if q not in recs:
                 rc = small.tile([P, 2], F32)
-                recs[m // 2] = rc
-            nc.vector.reciprocal(recs[m // 2][:, m % 2:m % 2 + n],
-                                 sums[m // 2][:, m % 2:m % 2 + n])
+                recs[q] = rc
+            nc.vector.reciprocal(recs[q][:, col:col + n], sums[q][:, col:col + n])
 
         def normalise(m, on_vector):
-            factor = recs[m // 2][:, m % 2:m % 2 + 1]
+            q, col = pair_column(m)
+            factor = recs[q][:, col:col + 1]
             if on_vector:
                 nc.vector.tensor_scalar(out=row(m), in0=row(m), scalar1=factor,
                                         scalar2=None, op0=ALU.mult)
@@ -218,11 +232,13 @@ def tile_guided_cam_module_pa_t_kernel(tc, x, query, out):
             load_unit(u)
 
         for n, hf in enumerate(HEAD_HALVES):
-            if n == FRAME_0_AT:
-                frame_energies(0)
+            if n in FRAME_0_AT:
+                half_energies(0, FRAME_0_AT.index(n))
             transposes(hf)
-            if 0 < n < FRAME_0_AT:
+            if 0 < n < FRAME_0_AT[1]:
                 quant_half(HEAD_HALVES[n - 1])
+            if n == FRAME_0_AT[0]:
+                first_passes(0)
             copy_out(hf, 0, False)
             copy_out(hf, 1, False)
         for u in range(RAW_BUFS, RAW_BUFS + HEAD_UNITS):
@@ -232,8 +248,6 @@ def tile_guided_cam_module_pa_t_kernel(tc, x, query, out):
             first = 2 * j
             second = 2 * j + 1
             unit = j + HEAD_UNITS
-            e_pair = e_pool.tile([P, 2, CH], F32)
-            e_tiles[j] = e_pair
             if j > 0:
                 frame_energies(j)
             if unit < UNITS:
@@ -242,12 +256,15 @@ def tile_guided_cam_module_pa_t_kernel(tc, x, query, out):
                 if unit + RAW_BUFS < UNITS:
                     load_unit(unit + RAW_BUFS)
             if unit <= UNITS:
-                if j > 1:
-                    reciprocal(first - 4, 2)
-                    finish(first - 4)
+                if j == 1:
+                    reciprocal(first - 2, 1)
+                    finish(first - 2)
+                elif j > 1:
+                    reciprocal(first - 3, 2)
                     finish(first - 3)
-                min_pass(first, 0)
-                min_pass(second, 0)
+                    finish(first - 2)
+                if j > 0:
+                    first_passes(j)
                 min_pass(first, 1)
                 exponent(first)
                 min_pass(second, 1)
@@ -261,13 +278,11 @@ def tile_guided_cam_module_pa_t_kernel(tc, x, query, out):
                     copy_out(hf, i, False)
             else:
                 if unit == UNITS + 1:
-                    reciprocal(first - 4, 2)
-                    finish(first - 4)
+                    reciprocal(first - 3, 1)
                     finish(first - 3)
-                min_pass(first, 0)
+                first_passes(j)
                 reciprocal(first - 2, 1)
                 finish(first - 2)
-                min_pass(second, 0)
                 min_pass(first, 1)
                 exponent(first)
                 reciprocal(second - 2, 1)

@@ -39,7 +39,7 @@ def tile_guided_cam_module_pa_t_kernel(tc, x, query, out):
         inp = ctx.enter_context(tc.tile_pool(name="inp", bufs=RAW_BUFS))
         grp_pool = ctx.enter_context(tc.tile_pool(name="grp", bufs=4))
         code_pool = ctx.enter_context(tc.tile_pool(name="code", bufs=8))
-        e_pool = ctx.enter_context(tc.tile_pool(name="e", bufs=7))
+        e_pool = ctx.enter_context(tc.tile_pool(name="e", bufs=9))
         small = ctx.enter_context(tc.tile_pool(name="small", bufs=8))
         tps = ctx.enter_context(tc.psum_pool(name="tps", bufs=4))
         eps = ctx.enter_context(tc.psum_pool(name="eps", bufs=4))
@@ -273,7 +273,8 @@ def tile_guided_cam_module_pa_t_kernel(tc, x, query, out):
                 vector_copies = VECTOR_COPIES[j % len(VECTOR_COPIES)]
                 for hf, i in banks[:vector_copies]:
                     copy_out(hf, i, True)
-                quant_unit(unit - 1)
+                if unit < UNITS:
+                    quant_unit(unit - 1)
                 for hf, i in banks[vector_copies:]:
                     copy_out(hf, i, False)
             else:
@@ -281,6 +282,8 @@ def tile_guided_cam_module_pa_t_kernel(tc, x, query, out):
                     reciprocal(first - 3, 1)
                     finish(first - 3)
                 first_passes(j)
+                if unit == UNITS + 1:
+                    quant_unit(UNITS - 1)
                 reciprocal(first - 2, 1)
                 finish(first - 2)
                 min_pass(first, 1)

@@ -28,7 +28,7 @@ HEAD_HALVES = (0, 2, 3, 4, 5, 1, 6, 7)
 FRAME_0_AT = (5, 7)
 HALF_UNITS = 3
 RAW_BUFS = 8
-VECTOR_COPIES = (1, 1, 0)
+VECTOR_COPIES = (1, 1, 1, 0)
 SINGLE_STORES_FROM = UNITS - HEAD_UNITS
 
 

@@ -178,10 +178,13 @@ def tile_guided_cam_module_pa_t_kernel(tc, x, query, out):
                 accum_out=mins[(m, h)][:],
             )
 
-        def first_passes(j):
+        def first_passes(j, finishing):
             e_pair = e_pool.tile([P, 2, CH], F32)
             e_tiles[j] = e_pair
             min_pass(2 * j, 0)
+            if finishing is not None:
+                reciprocal(finishing, 1)
+                finish(finishing)
             min_pass(2 * j + 1, 0)
 
         def pair_column(m):
@@ -238,7 +241,7 @@ def tile_guided_cam_module_pa_t_kernel(tc, x, query, out):
             if 0 < n < FRAME_0_AT[1]:
                 quant_half(HEAD_HALVES[n - 1])
             if n == FRAME_0_AT[0]:
-                first_passes(0)
+                first_passes(0, None)
             copy_out(hf, 0, False)
             copy_out(hf, 1, False)
         for u in range(RAW_BUFS, RAW_BUFS + HEAD_UNITS):
@@ -264,7 +267,7 @@ def tile_guided_cam_module_pa_t_kernel(tc, x, query, out):
                     finish(first - 3)
                     finish(first - 2)
                 if j > 0:
-                    first_passes(j)
+                    first_passes(j, None)
                 min_pass(first, 1)
                 exponent(first)
                 min_pass(second, 1)
@@ -281,11 +284,13 @@ def tile_guided_cam_module_pa_t_kernel(tc, x, query, out):
                 if unit == UNITS + 1:
                     reciprocal(first - 3, 1)
                     finish(first - 3)
-                first_passes(j)
-                if unit == UNITS + 1:
+                if unit > UNITS + 1:
+                    first_passes(j, first - 2)
+                else:
+                    first_passes(j, None)
                     quant_unit(UNITS - 1)
-                reciprocal(first - 2, 1)
-                finish(first - 2)
+                    reciprocal(first - 2, 1)
+                    finish(first - 2)
                 min_pass(first, 1)
                 exponent(first)
                 reciprocal(second - 2, 1)

from contextlib import ExitStack

import concourse.mybir as mybir
from concourse.masks import make_identity

F32 = mybir.dt.float32
BF16 = mybir.dt.bfloat16
U32 = mybir.dt.uint32
U8 = mybir.dt.uint8
FP8X4 = mybir.dt.float8_e4m3fn_x4
ALU = mybir.AluOpType
ACT = mybir.ActivationFunctionType

B = 4
P = 128
CH = 1024
K = 1024
FLOPS = 2 * B * CH * CH * K

BANK = 512
UNIT_COLS = 4 * K
UNITS = 4 * B
FRAMES = 4 * B
ROW_TILES = 2 * FRAMES

HEAD_UNITS = 4
HEAD_HALVES = (0, 2, 3, 4, 5, 1, 6, 7)
FRAME_0_AT = (5, 7)
HALF_UNITS = 3
RAW_BUFS = 8
VECTOR_COPIES = (1, 1, 1, 0)
SINGLE_STORES_FROM = UNITS - HEAD_UNITS


def tile_guided_cam_module_pa_t_kernel(tc, x, query, out):
    nc = tc.nc
    with ExitStack() as ctx:
        const = ctx.enter_context(tc.tile_pool(name="const", bufs=1))
        inp = ctx.enter_context(tc.tile_pool(name="inp", bufs=RAW_BUFS))
        grp_pool = ctx.enter_context(tc.tile_pool(name="grp", bufs=4))
        code_pool = ctx.enter_context(tc.tile_pool(name="code", bufs=8))
        e_pool = ctx.enter_context(tc.tile_pool(name="e", bufs=9))
        small = ctx.enter_context(tc.tile_pool(name="small", bufs=8))
        tps = ctx.enter_context(tc.psum_pool(name="tps", bufs=4))
        eps = ctx.enter_context(tc.psum_pool(name="eps", bufs=4))

        ident = const.tile([P, P], F32)
        make_identity(nc, ident[:])

        ctx.enter_context(tc.manual_schedule())

        raws = {}
        banks_of = {}
        grps = {}
        codes = {}
        scales = {}
        e_tiles = {}
        e_banks = {}
        mins = {}
        sums = {}
        recs = {}

        def dram_unit(u):
            b, q = divmod(u, 4)
            if q in (1, 2):
                return x[b].rearrange("(a p t) h w -> a p (t h w)", a=2, t=4)[q - 1]
            return query[b].rearrange("(p a t) h w -> a p (t h w)", a=2, t=4)[q // 3]

        def raw_tile(u):
            if u not in raws:
                raw = inp.tile([P, UNIT_COLS], BF16)
                raws[u] = raw
            return raws[u]

        def load_half(hf):
            u, s = divmod(hf, 2)
            cols = slice(s * 2 * K, (s + 1) * 2 * K)
            nc.sync.dma_start(out=raw_tile(u)[:, cols], in_=dram_unit(u)[:, cols])

        def load_unit(u):
            nc.sync.dma_start(out=raw_tile(u)[:], in_=dram_unit(u))

        def transposes(hf):
            u, s = divmod(hf, 2)
            words = raws[u][:].bitcast(F32)
            banks_of[hf] = []
            for t in (2 * s, 2 * s + 1):
                tp = tps.tile([P, 4, P], F32)
                for plane in range(4):
                    lo = t * (K // 2) + plane * P
                    nc.tensor.transpose(tp[:, plane, :], words[:, lo:lo + P], ident[:])
                banks_of[hf].append(tp)

        def copy_out(hf, i, on_vector):
            u, s = divmod(hf, 2)
            t = 2 * s + i
            if u not in grps:
                grp = grp_pool.tile([P, UNIT_COLS], BF16, align_bytes=64)
                grps[u] = grp
            words = grps[u][:].bitcast(F32)
            src = banks_of[hf][i][:].rearrange("p (g w) c -> p g c w", w=2)
            if u < HALF_UNITS:
                grouped = words.rearrange("p (s g c w) -> p s g c w", s=2, g=2, w=2)
                dst = grouped[:, s, :, i * P:(i + 1) * P, :]
            else:
                grouped = words.rearrange("p (g c w) -> p g c w", g=2, w=2)
                dst = grouped[:, :, t * P:(t + 1) * P, :]
            if on_vector:
                nc.vector.tensor_copy(out=dst, in_=src)
            else:
                nc.scalar.copy(out=dst, in_=src)

        def code_tiles(u):
            if u not in codes:
                cod = code_pool.tile([P, 2 * BANK], U32, align_bytes=64)
                scl = code_pool.tile([P, 2 * BANK], U8, align_bytes=64)
                codes[u] = cod
                scales[u] = scl
            return codes[u], scales[u]

        def quant_half(hf):
            u, s = divmod(hf, 2)
            cod, scl = code_tiles(u)
            for g in range(2):
                w = g * BANK + s * 2 * P
                lo = 4 * (s * BANK + g * 2 * P)
                nc.vector.quantize_mx(out=cod[:, w:w + 2 * P].bitcast(FP8X4),
                                      scales=scl[:, w:w + 2 * P],
                                      in_=grps[u][:, lo:lo + 4 * 2 * P])

        def quant_unit(u):
            cod, scl = code_tiles(u)
            nc.vector.quantize_mx(out=cod[:].bitcast(FP8X4), scales=scl[:], in_=grps[u][:])

        def energies(m, h):
            b, mm = divmod(m, 8)
            qu = 4 * b + 3 * (mm // 4)
            t = mm % 4
            xu = 4 * b + 1 + h
            ep = eps.tile([P, BANK], F32)
            for g in range(2):
                lo = g * BANK + t * P
                nc.tensor.matmul_mx(
                    out=ep[:],
                    lhsT=codes[qu][:, lo:lo + P].bitcast(FP8X4),
                    lhsT_scale=scales[qu][:, lo:lo + P],
                    rhs=codes[xu][:, g * BANK:(g + 1) * BANK].bitcast(FP8X4),
                    rhs_scale=scales[xu][:, g * BANK:(g + 1) * BANK],
                    start=(g == 0),
                    stop=(g == 1),
                )
            e_banks[(m, h)] = ep

        def half_energies(j, h):
            energies(2 * j, h)
            energies(2 * j + 1, h)

        def frame_energies(j):
            for h in range(2):
                half_energies(j, h)

        def row(m):
            return e_tiles[m // 2][:, m % 2, :]

        def min_pass(m, h):
            if h == 0:
                mn0 = small.tile([P, 1], F32)
                mins[(m, 0)] = mn0
                start_from = None
            else:
                mn = small.tile([P, 1], F32)
                mins[(m, 1)] = mn
                start_from = mins[(m, 0)][:]
            nc.vector.tensor_scalar(
                out=row(m)[:, h * BANK:(h + 1) * BANK].rearrange("p (c t) -> p c t", t=4),
                in0=e_banks[(m, h)][:].rearrange("p (t c) -> p c t", t=4),
                scalar1=1.0, scalar2=start_from, op0=ALU.mult, op1=ALU.min,
                accum_out=mins[(m, h)][:],
            )

        def first_passes(j, finishing):
            e_pair = e_pool.tile([P, 2, CH], F32)
            e_tiles[j] = e_pair
            min_pass(2 * j, 0)
            if finishing is not None:
                reciprocal(finishing, 1)
                finish(finishing)
            min_pass(2 * j + 1, 0)

        def pair_column(m):
            return divmod(m + 1, 2)

        def exponent(m):
            q, col = pair_column(m)
            if q not in sums:
                sm = small.tile([P, 2], F32)
                sums[q] = sm
            nc.scalar.activation(out=row(m), in_=row(m), func=ACT.Exp,
                                 bias=mins[(m, 1)][:], scale=-1.0,
                                 accum_out=sums[q][:, col:col + 1])

        def reciprocal(m, n):
            q, col = pair_column(m)
            if q not in recs:
                rc = small.tile([P, 2], F32)
                recs[q] = rc
            nc.vector.reciprocal(recs[q][:, col:col + n], sums[q][:, col:col + n])

        def normalise(m, on_vector):
            q, col = pair_column(m)
            factor = recs[q][:, col:col + 1]
            if on_vector:
                nc.vector.tensor_scalar(out=row(m), in0=row(m), scalar1=factor,
                                        scalar2=None, op0=ALU.mult)
            else:
                nc.gpsimd.tensor_scalar(out=row(m), in0=row(m), scalar1=factor,
                                        scalar2=0.0, op0=ALU.mult, op1=ALU.add)

        def store_rows(m, n):
            b, mm = divmod(m, 8)
            out_rows = out[b].rearrange("(p m) c -> p m c", m=8)
            nc.sync.dma_start(out=out_rows[:, mm:mm + n, :],
                              in_=e_tiles[m // 2][:, m % 2:m % 2 + n, :])

        def finish(m):
            normalise(m, False)
            if m // 2 >= SINGLE_STORES_FROM:
                store_rows(m, 1)
            elif m % 2 == 1:
                store_rows(m - 1, 2)

        for hf in HEAD_HALVES:
            load_half(hf)
        for u in range(HEAD_UNITS, RAW_BUFS):
            load_unit(u)

        for n, hf in enumerate(HEAD_HALVES):
            if n in FRAME_0_AT:
                half_energies(0, FRAME_0_AT.index(n))
            transposes(hf)
            if 0 < n < FRAME_0_AT[1]:
                quant_half(HEAD_HALVES[n - 1])
            if n == FRAME_0_AT[0]:
                first_passes(0, None)
            copy_out(hf, 0, False)
            copy_out(hf, 1, False)
        for u in range(RAW_BUFS, RAW_BUFS + HEAD_UNITS):
            load_unit(u)

        for j in range(FRAMES):
            first = 2 * j
            second = 2 * j + 1
            unit = j + HEAD_UNITS
            if j > 0:
                frame_energies(j)
            if unit < UNITS:
                transposes(2 * unit)
                transposes(2 * unit + 1)
                if unit + RAW_BUFS < UNITS:
                    load_unit(unit + RAW_BUFS)
            if unit <= UNITS:
                if j == 1:
                    reciprocal(first - 2, 1)
                    finish(first - 2)
                elif j > 1:
                    reciprocal(first - 3, 2)
                    finish(first - 3)
                    finish(first - 2)
                if j > 0:
                    first_passes(j, None)
                min_pass(first, 1)
                exponent(first)
                min_pass(second, 1)
                exponent(second)
                banks = [(2 * unit + s, i) for s in range(2) for i in range(2)] if unit < UNITS else []
                vector_copies = VECTOR_COPIES[j % len(VECTOR_COPIES)]
                for hf, i in banks[:vector_copies]:
                    copy_out(hf, i, True)
                if unit < UNITS:
                    quant_unit(unit - 1)
                for hf, i in banks[vector_copies:]:
                    copy_out(hf, i, False)
            else:
                if unit == UNITS + 1:
                    reciprocal(first - 3, 1)
                    finish(first - 3)
                if unit > UNITS + 1:
                    first_passes(j, first - 2)
                else:
                    first_passes(j, None)
                    quant_unit(UNITS - 1)
                    reciprocal(first - 2, 1)
                    finish(first - 2)
                min_pass(first, 1)
                exponent(first)
                reciprocal(second - 2, 1)
                finish(second - 2)
                min_pass(second, 1)
                exponent(second)

        for m in (ROW_TILES - 2, ROW_TILES - 1):
            reciprocal(m, 1)
            normalise(m, True)
            store_rows(m, 1)
